import numpy as np
import ml_dtypes

BF16 = ml_dtypes.bfloat16


def bf(x):
    return np.asarray(x, np.float32).astype(BF16)


def f32(x):
    return np.asarray(x, np.float32)


def f64(x):
    return np.asarray(x).astype(np.float64)


def striped(idx):
    return np.tile(idx.reshape(-1, 16).T, (8, 1))


S, D, M, N, P = 4096, 128, 256, 2048, 512
FLOOR = 0.5 / N
ERF_LIM, ERF_TERMS = 6.0, 150


def erf(a):
    c = np.clip(a, -ERF_LIM, ERF_LIM)
    term = c.copy()
    total = c.copy()
    for k in range(1, ERF_TERMS):
        term = term * (2.0 * c * c / (2 * k + 1))
        total = total + term
    r = 2.0 / np.sqrt(np.pi) * np.exp(-c * c) * total
    return np.where(np.abs(a) > ERF_LIM, np.sign(a), r)


def gelu(v):
    return 0.5 * v * (1.0 + erf(v / np.sqrt(2.0)))


def setup_inputs():
    return {"table": bf(np.random.standard_normal((S, D))), "w0": bf(2.0 * np.random.standard_normal((D, M)) / np.sqrt(D)), "b0": f32(0.1 * np.random.standard_normal((M, 1))), "adj_t": bf(FLOOR + np.random.random((N, N)) ** P), "mask": f32(np.random.random((1, N)) > 0.2), "w1": bf(3.0 * np.random.standard_normal((M, M)) / np.sqrt(M)), "b1": f32(0.1 * np.random.standard_normal((M, 1))), "w2": bf(3.0 * np.random.standard_normal((M, M)) / np.sqrt(M)), "b2": f32(0.1 * np.random.standard_normal((M, 1))), "offs": striped(np.random.permutation(S)[:N])}


def reference(table, w0, b0, adj_t, mask, w1, b1, w2, b2, offs):
    idx = offs[:16].T.reshape(-1)
    a = f64(adj_t)
    scale = f64(mask) / a.sum(axis=0, keepdims=True)
    h = f64(w0).T @ f64(table)[idx].T + f64(b0)
    y = gelu((h @ a) * scale)
    h = f64(w1).T @ y + f64(b1)
    y = gelu((h @ a) * scale)
    h = f64(w2).T @ y + f64(b2)
    return gelu((h @ a) * scale)

@@ -1,0 +1,146 @@
+import concourse.mybir as mybir
+from concourse.masks import make_identity
+
+BF16, F32, U16 = mybir.dt.bfloat16, mybir.dt.float32, mybir.dt.uint16
+ACT = mybir.ActivationFunctionType
+ADD = mybir.AluOpType.add
+
+P = 128
+S = 4096
+M = 256
+N = 2048
+PIECE = 512
+WORD_BLOCKS = S // P
+NODE_BLOCKS = N // P
+FEAT_BLOCKS = M // P
+PIECES = N // PIECE
+BLOCKS_A_PIECE = PIECE // P
+LAYERS = 3
+
+FLOPS = 2 * P * M * N + 2 * 2 * M * M * N + LAYERS * 2 * M * N * N
+
+
+def tile_graphconvlayer_b_kernel(tc, table, w0, b0, adj_t, mask, w1, b1, w2, b2, offs, out):
+    nc = tc.nc
+    with (
+        tc.tile_pool(name="held", bufs=1) as held,
+        tc.tile_pool(name="layer", bufs=2) as layer,
+        tc.tile_pool(name="work", bufs=3) as work,
+        tc.psum_pool(name="psum_acc", bufs=4) as psum_acc,
+        tc.psum_pool(name="psum_flip", bufs=2) as psum_flip,
+        tc.psum_pool(name="psum_lin", bufs=2) as psum_lin,
+    ):
+        offsets = held.tile([P, N // 16], U16, name="offsets")
+        nc.sync.dma_start(offsets[:], offs)
+
+        table_rows = held.tile([P, WORD_BLOCKS, P], BF16, name="table_rows")
+        table_blocks = table.rearrange("(b q) d -> q b d", q=P)
+        for g in range(4):
+            nc.sync.dma_start(table_rows[:, 8 * g : 8 * g + 8, :], table_blocks[:, 8 * g : 8 * g + 8, :])
+
+        w0_sb = held.tile([P, M], BF16, name="w0_sb")
+        nc.sync.dma_start(w0_sb[:], w0)
+        b0_cols = [held.tile([P, 1], F32, name=f"b0_col{e}") for e in range(FEAT_BLOCKS)]
+        for e in range(FEAT_BLOCKS):
+            nc.sync.dma_start(b0_cols[e][:], b0[e * P : (e + 1) * P, :])
+
+        adj = [held.tile([P, NODE_BLOCKS, PIECE], BF16, name=f"adj{p}") for p in range(PIECES)]
+        adj_blocks = adj_t.rearrange("(b q) n -> q b n", q=P)
+
+        def load_adj(p):
+            for g in range(4):
+                nc.sync.dma_start(
+                    adj[p][:, 4 * g : 4 * g + 4, :],
+                    adj_blocks[:, 4 * g : 4 * g + 4, p * PIECE : (p + 1) * PIECE],
+                )
+
+        load_adj(0)
+        mask_all = held.tile([P, N], F32, name="mask_all")
+        nc.sync.dma_start(mask_all[:], mask.rearrange("o n -> (o n)").partition_broadcast(P))
+        weights, biases = {}, {}
+        for l, (w, b) in ((1, (w1, b1)), (2, (w2, b2))):
+            weights[l] = held.tile([P, FEAT_BLOCKS, M], BF16, name=f"w{l}_sb")
+            nc.sync.dma_start(weights[l][:], w.rearrange("(k q) e -> q k e", q=P))
+            biases[l] = held.tile([P, M], F32, name=f"b{l}_all")
+            nc.sync.dma_start(biases[l][:], b.rearrange("m o -> (m o)").partition_broadcast(P))
+            load_adj(l)
+        load_adj(3)
+
+        identity = held.tile([P, P], BF16, name="identity")
+        make_identity(nc, identity[:])
+        ones = held.tile([P, P], BF16, name="ones")
+        nc.vector.memset(ones[:], 1.0)
+
+        table_t = held.tile([P, S], BF16, name="table_t")
+        for g in range(4):
+            flipped = psum_flip.tile([P, 8 * P], BF16, tag="flipped")
+            for k in range(8):
+                nc.tensor.transpose(flipped[:, k * P : (k + 1) * P], table_rows[:, 8 * g + k, :], identity[:])
+            nc.vector.tensor_copy(table_t[:, g * 8 * P : (g + 1) * 8 * P], flipped[:])
+
+        h_t = layer.tile([P, NODE_BLOCKS, M], BF16, tag="h_t")
+        for p in range(PIECES):
+            flipped = psum_flip.tile([P, BLOCKS_A_PIECE, M], BF16, tag="flipped")
+            for e in range(FEAT_BLOCKS):
+                looked_up = table_t[:].indirect(offsets[:, p * (PIECE // 16) : (p + 1) * (PIECE // 16)])
+                product = psum_acc.tile([P, PIECE], F32, tag="acc")
+                nc.tensor.matmul(product[:], w0_sb[:, e * P : (e + 1) * P], looked_up, start=True, stop=True)
+                h0 = work.tile([P, PIECE], BF16, tag="h0")
+                nc.scalar.activation(h0[:], product[:], ACT.Identity, bias=b0_cols[e][:])
+                for k in range(BLOCKS_A_PIECE):
+                    nc.tensor.transpose(flipped[:, k, e * P : (e + 1) * P], h0[:, k * P : (k + 1) * P], identity[:])
+            nc.vector.tensor_copy(h_t[:, p * BLOCKS_A_PIECE : (p + 1) * BLOCKS_A_PIECE, :], flipped[:])
+
+        scale = held.tile([P, N], F32, name="scale")
+
+        def degree(p):
+            columns = slice(p * PIECE, (p + 1) * PIECE)
+            deg = psum_acc.tile([P, PIECE], F32, tag="acc")
+            for b in range(NODE_BLOCKS):
+                nc.tensor.matmul(deg[:], ones[:], adj[p][:, b, :], start=(b == 0), stop=(b == NODE_BLOCKS - 1))
+            nc.vector.reciprocal(scale[:, columns], deg[:])
+            nc.vector.tensor_mul(scale[:, columns], scale[:, columns], mask_all[:, columns])
+
+        def aggregate(l, p, h_t, y):
+            columns = slice(p * PIECE, (p + 1) * PIECE)
+            for e in range(FEAT_BLOCKS):
+                acc = psum_acc.tile([P, PIECE], F32, tag="acc")
+                for b in range(NODE_BLOCKS):
+                    nc.tensor.matmul(
+                        acc[:], h_t[:, b, e * P : (e + 1) * P], adj[p][:, b, :],
+                        start=(b == 0), stop=(b == NODE_BLOCKS - 1),
+                    )
+                scaled = work.tile([P, PIECE], F32, tag="scaled")
+                nc.vector.tensor_mul(scaled[:], acc[:], scale[:, columns])
+                if l < LAYERS - 1:
+                    nc.scalar.activation(y[:, e, columns], scaled[:], ACT.Gelu)
+                else:
+                    result = work.tile([P, PIECE], F32, tag="result")
+                    nc.scalar.activation(result[:], scaled[:], ACT.Gelu)
+                    nc.sync.dma_start(out[e * P : (e + 1) * P, columns], result[:])
+
+        def linear(l, p, y, h_t):
+            for b in range(p * BLOCKS_A_PIECE, (p + 1) * BLOCKS_A_PIECE, 2):
+                pair = psum_lin.tile([P, 2, M], F32, tag="pair")
+                for i in range(2):
+                    for k in range(FEAT_BLOCKS):
+                        nc.tensor.matmul(
+                            pair[:, i, :], y[:, k, (b + i) * P : (b + i + 1) * P], weights[l][:, k, :],
+                            start=(k == 0), stop=(k == FEAT_BLOCKS - 1),
+                        )
+                bias = biases[l][:].unsqueeze(1).to_broadcast([P, 2, M])
+                nc.vector.tensor_tensor(h_t[:, b : b + 2, :], pair[:], bias, ADD)
+
+        for l in range(LAYERS):
+            last = l == LAYERS - 1
+            y = None if last else layer.tile([P, FEAT_BLOCKS, N], BF16, name="y", tag="y")
+            next_h_t = None if last else layer.tile([P, NODE_BLOCKS, M], BF16, name="h_t", tag="h_t")
+            for p in range(PIECES):
+                if l == 0:
+                    degree(p)
+                aggregate(l, p, h_t, y)
+                if not last and p > 0:
+                    linear(l + 1, p - 1, y, next_h_t)
+            if not last:
+                linear(l + 1, PIECES - 1, y, next_h_t)
+            h_t = next_h_t

@@ -26,9 +26,8 @@ def tile_graphconvlayer_b_kernel(tc, table, w0, b0, adj_t, mask, w1, b1, w2, b2,
         tc.tile_pool(name="held", bufs=1) as held,
         tc.tile_pool(name="layer", bufs=2) as layer,
         tc.tile_pool(name="work", bufs=3) as work,
-        tc.psum_pool(name="psum_acc", bufs=4) as psum_acc,
-        tc.psum_pool(name="psum_flip", bufs=2) as psum_flip,
-        tc.psum_pool(name="psum_lin", bufs=2) as psum_lin,
+        tc.psum_pool(name="psum_acc", bufs=6) as psum_acc,
+        tc.psum_pool(name="psum_aux", bufs=2) as psum_aux,
     ):
         offsets = held.tile([P, N // 16], U16, name="offsets")
         nc.sync.dma_start(offsets[:], offs)
@@ -55,6 +54,7 @@ def tile_graphconvlayer_b_kernel(tc, table, w0, b0, adj_t, mask, w1, b1, w2, b2,
                 )
 
         load_adj(0)
+        load_adj(1)
         mask_all = held.tile([P, N], F32, name="mask_all")
         nc.sync.dma_start(mask_all[:], mask.rearrange("o n -> (o n)").partition_broadcast(P))
         weights, biases = {}, {}
@@ -63,24 +63,23 @@ def tile_graphconvlayer_b_kernel(tc, table, w0, b0, adj_t, mask, w1, b1, w2, b2,
             nc.sync.dma_start(weights[l][:], w.rearrange("(k q) e -> q k e", q=P))
             biases[l] = held.tile([P, M], F32, name=f"b{l}_all")
             nc.sync.dma_start(biases[l][:], b.rearrange("m o -> (m o)").partition_broadcast(P))
-            load_adj(l)
-        load_adj(3)
+            load_adj(l + 1)
 
         identity = held.tile([P, P], BF16, name="identity")
         make_identity(nc, identity[:])
-        ones = held.tile([P, P], BF16, name="ones")
+        ones = held.tile([P, P], F32, name="ones")
         nc.vector.memset(ones[:], 1.0)
 
         table_t = held.tile([P, S], BF16, name="table_t")
         for g in range(4):
-            flipped = psum_flip.tile([P, 8 * P], BF16, tag="flipped")
+            flipped = psum_aux.tile([P, 8 * P], BF16, tag="aux")
             for k in range(8):
                 nc.tensor.transpose(flipped[:, k * P : (k + 1) * P], table_rows[:, 8 * g + k, :], identity[:])
             nc.vector.tensor_copy(table_t[:, g * 8 * P : (g + 1) * 8 * P], flipped[:])
 
         h_t = layer.tile([P, NODE_BLOCKS, M], BF16, tag="h_t")
         for p in range(PIECES):
-            flipped = psum_flip.tile([P, BLOCKS_A_PIECE, M], BF16, tag="flipped")
+            flipped = psum_aux.tile([P, BLOCKS_A_PIECE, M], BF16, tag="aux")
             for e in range(FEAT_BLOCKS):
                 looked_up = table_t[:].indirect(offsets[:, p * (PIECE // 16) : (p + 1) * (PIECE // 16)])
                 product = psum_acc.tile([P, PIECE], F32, tag="acc")
@@ -95,9 +94,14 @@ def tile_graphconvlayer_b_kernel(tc, table, w0, b0, adj_t, mask, w1, b1, w2, b2,
 
         def degree(p):
             columns = slice(p * PIECE, (p + 1) * PIECE)
+            part = work.tile([P, 4, PIECE], F32, tag="part")
+            nc.vector.tensor_tensor(part[:], adj[p][:, 0:4, :], adj[p][:, 4:8, :], ADD)
+            nc.vector.tensor_tensor(part[:], part[:], adj[p][:, 8:12, :], ADD)
+            nc.vector.tensor_tensor(part[:], part[:], adj[p][:, 12:16, :], ADD)
+            nc.vector.tensor_tensor(part[:, 0:2, :], part[:, 0:2, :], part[:, 2:4, :], ADD)
+            nc.vector.tensor_tensor(part[:, 0, :], part[:, 0, :], part[:, 1, :], ADD)
             deg = psum_acc.tile([P, PIECE], F32, tag="acc")
-            for b in range(NODE_BLOCKS):
-                nc.tensor.matmul(deg[:], ones[:], adj[p][:, b, :], start=(b == 0), stop=(b == NODE_BLOCKS - 1))
+            nc.tensor.matmul(deg[:], ones[:], part[:, 0, :], start=True, stop=True)
             nc.vector.reciprocal(scale[:, columns], deg[:])
             nc.vector.tensor_mul(scale[:, columns], scale[:, columns], mask_all[:, columns])
 
@@ -121,7 +125,7 @@ def tile_graphconvlayer_b_kernel(tc, table, w0, b0, adj_t, mask, w1, b1, w2, b2,
 
         def linear(l, p, y, h_t):
             for b in range(p * BLOCKS_A_PIECE, (p + 1) * BLOCKS_A_PIECE, 2):
-                pair = psum_lin.tile([P, 2, M], F32, tag="pair")
+                pair = psum_aux.tile([P, 2, M], F32, tag="aux")
                 for i in range(2):
                     for k in range(FEAT_BLOCKS):
                         nc.tensor.matmul(

@@ -16,6 +16,7 @@ FEAT_BLOCKS = M // P
 PIECES = N // PIECE
 BLOCKS_A_PIECE = PIECE // P
 LAYERS = 3
+H_ROW = 272
 
 FLOPS = 2 * P * M * N + 2 * 2 * M * M * N + LAYERS * 2 * M * N * N
 
@@ -25,12 +26,17 @@ def tile_graphconvlayer_b_kernel(tc, table, w0, b0, adj_t, mask, w1, b1, w2, b2,
     with (
         tc.tile_pool(name="held", bufs=1) as held,
         tc.tile_pool(name="layer", bufs=2) as layer,
-        tc.tile_pool(name="work", bufs=3) as work,
-        tc.psum_pool(name="psum_acc", bufs=6) as psum_acc,
-        tc.psum_pool(name="psum_aux", bufs=2) as psum_aux,
+        tc.tile_pool(name="work", bufs=4) as work,
+        tc.psum_pool(name="psum_acc", bufs=4) as psum_acc,
+        tc.psum_pool(name="psum_aux", bufs=4) as psum_aux,
     ):
         offsets = held.tile([P, N // 16], U16, name="offsets")
         nc.sync.dma_start(offsets[:], offs)
+
+        rows = held.tile([P, P], F32, name="rows")
+        nc.vector.memset(rows[:], 0.0)
+        nc.sync.dma_start(rows[0:NODE_BLOCKS, :], mask.rearrange("o (b q) -> (o b) q", q=P))
+        nc.sync.dma_start(rows[NODE_BLOCKS : NODE_BLOCKS + FEAT_BLOCKS, :], b0.rearrange("(e q) o -> e (q o)", q=P))
 
         table_rows = held.tile([P, WORD_BLOCKS, P], BF16, name="table_rows")
         table_blocks = table.rearrange("(b q) d -> q b d", q=P)
@@ -39,9 +45,6 @@ def tile_graphconvlayer_b_kernel(tc, table, w0, b0, adj_t, mask, w1, b1, w2, b2,
 
         w0_sb = held.tile([P, M], BF16, name="w0_sb")
         nc.sync.dma_start(w0_sb[:], w0)
-        b0_cols = [held.tile([P, 1], F32, name=f"b0_col{e}") for e in range(FEAT_BLOCKS)]
-        for e in range(FEAT_BLOCKS):
-            nc.sync.dma_start(b0_cols[e][:], b0[e * P : (e + 1) * P, :])
 
         adj = [held.tile([P, NODE_BLOCKS, PIECE], BF16, name=f"adj{p}") for p in range(PIECES)]
         adj_blocks = adj_t.rearrange("(b q) n -> q b n", q=P)
@@ -55,8 +58,6 @@ def tile_graphconvlayer_b_kernel(tc, table, w0, b0, adj_t, mask, w1, b1, w2, b2,
 
         load_adj(0)
         load_adj(1)
-        mask_all = held.tile([P, N], F32, name="mask_all")
-        nc.sync.dma_start(mask_all[:], mask.rearrange("o n -> (o n)").partition_broadcast(P))
         weights, biases = {}, {}
         for l, (w, b) in ((1, (w1, b1)), (2, (w2, b2))):
             weights[l] = held.tile([P, FEAT_BLOCKS, M], BF16, name=f"w{l}_sb")
@@ -65,63 +66,54 @@ def tile_graphconvlayer_b_kernel(tc, table, w0, b0, adj_t, mask, w1, b1, w2, b2,
             nc.sync.dma_start(biases[l][:], b.rearrange("m o -> (m o)").partition_broadcast(P))
             load_adj(l + 1)
 
-        identity = held.tile([P, P], BF16, name="identity")
-        make_identity(nc, identity[:])
-        ones = held.tile([P, P], F32, name="ones")
-        nc.vector.memset(ones[:], 1.0)
+        identity_bf16 = held.tile([P, P], BF16, name="identity_bf16")
+        make_identity(nc, identity_bf16[:])
+        identity_f32 = held.tile([P, P], F32, name="identity_f32")
+        make_identity(nc, identity_f32[:])
+
+        flipped_rows = psum_aux.tile([P, P], F32, tag="aux")
+        nc.tensor.transpose(flipped_rows[:], rows[:], identity_f32[:])
+        columns = held.tile([P, NODE_BLOCKS + FEAT_BLOCKS], F32, name="columns")
+        nc.vector.tensor_copy(columns[:], flipped_rows[:, 0 : NODE_BLOCKS + FEAT_BLOCKS])
 
         table_t = held.tile([P, S], BF16, name="table_t")
         for g in range(4):
-            flipped = psum_aux.tile([P, 8 * P], BF16, tag="aux")
+            flipped_words = psum_aux.tile([P, 8 * P], BF16, tag="aux")
             for k in range(8):
-                nc.tensor.transpose(flipped[:, k * P : (k + 1) * P], table_rows[:, 8 * g + k, :], identity[:])
-            nc.vector.tensor_copy(table_t[:, g * 8 * P : (g + 1) * 8 * P], flipped[:])
+                nc.tensor.transpose(flipped_words[:, k * P : (k + 1) * P], table_rows[:, 8 * g + k, :], identity_bf16[:])
+            nc.vector.tensor_copy(table_t[:, g * 8 * P : (g + 1) * 8 * P], flipped_words[:])
 
-        h_t = layer.tile([P, NODE_BLOCKS, M], BF16, tag="h_t")
+        h_t = layer.tile([P, NODE_BLOCKS, H_ROW], BF16, tag="h_t")
+        nc.vector.memset(h_t[:, :, M : M + 1], 1.0)
         for p in range(PIECES):
-            flipped = psum_aux.tile([P, BLOCKS_A_PIECE, M], BF16, tag="aux")
+            flipped_h = psum_aux.tile([P, BLOCKS_A_PIECE, M], BF16, tag="aux")
             for e in range(FEAT_BLOCKS):
                 looked_up = table_t[:].indirect(offsets[:, p * (PIECE // 16) : (p + 1) * (PIECE // 16)])
                 product = psum_acc.tile([P, PIECE], F32, tag="acc")
                 nc.tensor.matmul(product[:], w0_sb[:, e * P : (e + 1) * P], looked_up, start=True, stop=True)
                 h0 = work.tile([P, PIECE], BF16, tag="h0")
-                nc.scalar.activation(h0[:], product[:], ACT.Identity, bias=b0_cols[e][:])
+                nc.scalar.activation(
+                    h0[:], product[:], ACT.Identity, bias=columns[:, NODE_BLOCKS + e : NODE_BLOCKS + e + 1]
+                )
                 for k in range(BLOCKS_A_PIECE):
-                    nc.tensor.transpose(flipped[:, k, e * P : (e + 1) * P], h0[:, k * P : (k + 1) * P], identity[:])
-            nc.vector.tensor_copy(h_t[:, p * BLOCKS_A_PIECE : (p + 1) * BLOCKS_A_PIECE, :], flipped[:])
+                    nc.tensor.transpose(flipped_h[:, k, e * P : (e + 1) * P], h0[:, k * P : (k + 1) * P], identity_bf16[:])
+            nc.vector.tensor_copy(h_t[:, p * BLOCKS_A_PIECE : (p + 1) * BLOCKS_A_PIECE, 0:M], flipped_h[:])
 
-        scale = held.tile([P, N], F32, name="scale")
+        scale_t = held.tile([P, NODE_BLOCKS], F32, name="scale_t")
 
-        def degree(p):
-            columns = slice(p * PIECE, (p + 1) * PIECE)
-            part = work.tile([P, 4, PIECE], F32, tag="part")
-            nc.vector.tensor_tensor(part[:], adj[p][:, 0:4, :], adj[p][:, 4:8, :], ADD)
-            nc.vector.tensor_tensor(part[:], part[:], adj[p][:, 8:12, :], ADD)
-            nc.vector.tensor_tensor(part[:], part[:], adj[p][:, 12:16, :], ADD)
-            nc.vector.tensor_tensor(part[:, 0:2, :], part[:, 0:2, :], part[:, 2:4, :], ADD)
-            nc.vector.tensor_tensor(part[:, 0, :], part[:, 0, :], part[:, 1, :], ADD)
-            deg = psum_acc.tile([P, PIECE], F32, tag="acc")
-            nc.tensor.matmul(deg[:], ones[:], part[:, 0, :], start=True, stop=True)
-            nc.vector.reciprocal(scale[:, columns], deg[:])
-            nc.vector.tensor_mul(scale[:, columns], scale[:, columns], mask_all[:, columns])
-
-        def aggregate(l, p, h_t, y):
-            columns = slice(p * PIECE, (p + 1) * PIECE)
-            for e in range(FEAT_BLOCKS):
-                acc = psum_acc.tile([P, PIECE], F32, tag="acc")
-                for b in range(NODE_BLOCKS):
-                    nc.tensor.matmul(
-                        acc[:], h_t[:, b, e * P : (e + 1) * P], adj[p][:, b, :],
-                        start=(b == 0), stop=(b == NODE_BLOCKS - 1),
-                    )
-                scaled = work.tile([P, PIECE], F32, tag="scaled")
-                nc.vector.tensor_mul(scaled[:], acc[:], scale[:, columns])
-                if l < LAYERS - 1:
-                    nc.scalar.activation(y[:, e, columns], scaled[:], ACT.Gelu)
-                else:
-                    result = work.tile([P, PIECE], F32, tag="result")
-                    nc.scalar.activation(result[:], scaled[:], ACT.Gelu)
-                    nc.sync.dma_start(out[e * P : (e + 1) * P, columns], result[:])
+        def aggregate(l, b, h_t, y_t):
+            p, j = divmod(b, BLOCKS_A_PIECE)
+            width = M + 1 if l == 0 else M
+            acc = psum_acc.tile([P, M + 1], F32, tag="acc")
+            for i in range(NODE_BLOCKS):
+                nc.tensor.matmul(
+                    acc[:, 0:width], adj[p][:, i, j * P : (j + 1) * P], h_t[:, i, 0:width],
+                    start=(i == 0), stop=(i == NODE_BLOCKS - 1),
+                )
+            if l == 0:
+                nc.vector.reciprocal(scale_t[:, b : b + 1], acc[:, M : M + 1])
+                nc.vector.tensor_mul(scale_t[:, b : b + 1], scale_t[:, b : b + 1], columns[:, b : b + 1])
+            nc.scalar.activation(y_t[:], acc[:, 0:M], ACT.Gelu, scale=scale_t[:, b : b + 1])
 
         def linear(l, p, y, h_t):
             for b in range(p * BLOCKS_A_PIECE, (p + 1) * BLOCKS_A_PIECE, 2):
@@ -133,18 +125,29 @@ def tile_graphconvlayer_b_kernel(tc, table, w0, b0, adj_t, mask, w1, b1, w2, b2,
                             start=(k == 0), stop=(k == FEAT_BLOCKS - 1),
                         )
                 bias = biases[l][:].unsqueeze(1).to_broadcast([P, 2, M])
-                nc.vector.tensor_tensor(h_t[:, b : b + 2, :], pair[:], bias, ADD)
+                nc.vector.tensor_tensor(h_t[:, b : b + 2, 0:M], pair[:], bias, ADD)
 
         for l in range(LAYERS):
             last = l == LAYERS - 1
+            y_dtype = F32 if last else BF16
+            y_identity = identity_f32 if last else identity_bf16
             y = None if last else layer.tile([P, FEAT_BLOCKS, N], BF16, name="y", tag="y")
-            next_h_t = None if last else layer.tile([P, NODE_BLOCKS, M], BF16, name="h_t", tag="h_t")
+            next_h_t = None if last else layer.tile([P, NODE_BLOCKS, H_ROW], BF16, name="h_t", tag="h_t")
             for p in range(PIECES):
-                if l == 0:
-                    degree(p)
-                aggregate(l, p, h_t, y)
-                if not last and p > 0:
-                    linear(l + 1, p - 1, y, next_h_t)
-            if not last:
-                linear(l + 1, PIECES - 1, y, next_h_t)
+                piece = slice(p * PIECE, (p + 1) * PIECE)
+                flipped_y = [psum_aux.tile([P, PIECE], y_dtype, name=f"flipped_y{k}", tag="aux") for k in range(FEAT_BLOCKS)]
+                for j in range(BLOCKS_A_PIECE):
+                    y_t = work.tile([P, M], y_dtype, name="y_t", tag=("y_t_last" if last else "y_t"))
+                    aggregate(l, p * BLOCKS_A_PIECE + j, h_t, y_t)
+                    for k in range(FEAT_BLOCKS):
+                        nc.tensor.transpose(flipped_y[k][:, j * P : (j + 1) * P], y_t[:, k * P : (k + 1) * P], y_identity[:])
+                for k in range(FEAT_BLOCKS):
+                    if last:
+                        result = work.tile([P, PIECE], F32, tag="result")
+                        nc.vector.tensor_copy(result[:], flipped_y[k][:])
+                        nc.sync.dma_start(out[k * P : (k + 1) * P, piece], result[:])
+                    else:
+                        nc.vector.tensor_copy(y[:, k, piece], flipped_y[k][:])
+                if not last:
+                    linear(l + 1, p, y, next_h_t)
             h_t = next_h_t

@@ -30,6 +30,11 @@ def tile_graphconvlayer_b_kernel(tc, table, w0, b0, adj_t, mask, w1, b1, w2, b2,
         tc.psum_pool(name="psum_acc", bufs=4) as psum_acc,
         tc.psum_pool(name="psum_aux", bufs=4) as psum_aux,
     ):
+        table_rows = held.tile([P, WORD_BLOCKS, P], BF16, name="table_rows")
+        table_blocks = table.rearrange("(b q) d -> q b d", q=P)
+        for g in range(WORD_BLOCKS // 4):
+            nc.sync.dma_start(table_rows[:, 4 * g : 4 * g + 4, :], table_blocks[:, 4 * g : 4 * g + 4, :])
+
         offsets = held.tile([P, N // 16], U16, name="offsets")
         nc.sync.dma_start(offsets[:], offs)
 
@@ -37,11 +42,6 @@ def tile_graphconvlayer_b_kernel(tc, table, w0, b0, adj_t, mask, w1, b1, w2, b2,
         nc.vector.memset(rows[:], 0.0)
         nc.sync.dma_start(rows[0:NODE_BLOCKS, :], mask.rearrange("o (b q) -> (o b) q", q=P))
         nc.sync.dma_start(rows[NODE_BLOCKS : NODE_BLOCKS + FEAT_BLOCKS, :], b0.rearrange("(e q) o -> e (q o)", q=P))
-
-        table_rows = held.tile([P, WORD_BLOCKS, P], BF16, name="table_rows")
-        table_blocks = table.rearrange("(b q) d -> q b d", q=P)
-        for g in range(4):
-            nc.sync.dma_start(table_rows[:, 8 * g : 8 * g + 8, :], table_blocks[:, 8 * g : 8 * g + 8, :])
 
         w0_sb = held.tile([P, M], BF16, name="w0_sb")
         nc.sync.dma_start(w0_sb[:], w0)
@@ -71,33 +71,42 @@ def tile_graphconvlayer_b_kernel(tc, table, w0, b0, adj_t, mask, w1, b1, w2, b2,
         identity_f32 = held.tile([P, P], F32, name="identity_f32")
         make_identity(nc, identity_f32[:])
 
+        table_t = held.tile([P, S], BF16, name="table_t")
+        for g in range(WORD_BLOCKS // 4):
+            flipped_words = psum_aux.tile([P, 4 * P], BF16, tag="aux")
+            for k in range(4):
+                nc.tensor.transpose(flipped_words[:, k * P : (k + 1) * P], table_rows[:, 4 * g + k, :], identity_bf16[:])
+            if g % 2 == 0:
+                nc.vector.tensor_copy(table_t[:, g * 4 * P : (g + 1) * 4 * P], flipped_words[:])
+            else:
+                nc.scalar.copy(table_t[:, g * 4 * P : (g + 1) * 4 * P], flipped_words[:])
+
         flipped_rows = psum_aux.tile([P, P], F32, tag="aux")
         nc.tensor.transpose(flipped_rows[:], rows[:], identity_f32[:])
         columns = held.tile([P, NODE_BLOCKS + FEAT_BLOCKS], F32, name="columns")
         nc.vector.tensor_copy(columns[:], flipped_rows[:, 0 : NODE_BLOCKS + FEAT_BLOCKS])
 
-        table_t = held.tile([P, S], BF16, name="table_t")
-        for g in range(4):
-            flipped_words = psum_aux.tile([P, 8 * P], BF16, tag="aux")
-            for k in range(8):
-                nc.tensor.transpose(flipped_words[:, k * P : (k + 1) * P], table_rows[:, 8 * g + k, :], identity_bf16[:])
-            nc.vector.tensor_copy(table_t[:, g * 8 * P : (g + 1) * 8 * P], flipped_words[:])
-
         h_t = layer.tile([P, NODE_BLOCKS, H_ROW], BF16, tag="h_t")
         nc.vector.memset(h_t[:, :, M : M + 1], 1.0)
-        for p in range(PIECES):
-            flipped_h = psum_aux.tile([P, BLOCKS_A_PIECE, M], BF16, tag="aux")
-            for e in range(FEAT_BLOCKS):
-                looked_up = table_t[:].indirect(offsets[:, p * (PIECE // 16) : (p + 1) * (PIECE // 16)])
-                product = psum_acc.tile([P, PIECE], F32, tag="acc")
-                nc.tensor.matmul(product[:], w0_sb[:, e * P : (e + 1) * P], looked_up, start=True, stop=True)
-                h0 = work.tile([P, PIECE], BF16, tag="h0")
-                nc.scalar.activation(
-                    h0[:], product[:], ACT.Identity, bias=columns[:, NODE_BLOCKS + e : NODE_BLOCKS + e + 1]
-                )
-                for k in range(BLOCKS_A_PIECE):
-                    nc.tensor.transpose(flipped_h[:, k, e * P : (e + 1) * P], h0[:, k * P : (k + 1) * P], identity_bf16[:])
-            nc.vector.tensor_copy(h_t[:, p * BLOCKS_A_PIECE : (p + 1) * BLOCKS_A_PIECE, 0:M], flipped_h[:])
+        h0 = {}
+        for p in range(PIECES + 1):
+            if p < PIECES:
+                for e in range(FEAT_BLOCKS):
+                    looked_up = table_t[:].indirect(offsets[:, p * (PIECE // 16) : (p + 1) * (PIECE // 16)])
+                    product = psum_acc.tile([P, PIECE], F32, tag="acc")
+                    nc.tensor.matmul(product[:], w0_sb[:, e * P : (e + 1) * P], looked_up, start=True, stop=True)
+                    h0[p, e] = work.tile([P, PIECE], BF16, name="h0", tag="h0")
+                    nc.scalar.activation(
+                        h0[p, e][:], product[:], ACT.Identity, bias=columns[:, NODE_BLOCKS + e : NODE_BLOCKS + e + 1]
+                    )
+            if p >= 1:
+                flipped_h = psum_aux.tile([P, BLOCKS_A_PIECE, M], BF16, tag="aux")
+                for e in range(FEAT_BLOCKS):
+                    for k in range(BLOCKS_A_PIECE):
+                        nc.tensor.transpose(
+                            flipped_h[:, k, e * P : (e + 1) * P], h0[p - 1, e][:, k * P : (k + 1) * P], identity_bf16[:]
+                        )
+                nc.vector.tensor_copy(h_t[:, (p - 1) * BLOCKS_A_PIECE : p * BLOCKS_A_PIECE, 0:M], flipped_h[:])
 
         scale_t = held.tile([P, NODE_BLOCKS], F32, name="scale_t")
 
@@ -133,21 +142,28 @@ def tile_graphconvlayer_b_kernel(tc, table, w0, b0, adj_t, mask, w1, b1, w2, b2,
             y_identity = identity_f32 if last else identity_bf16
             y = None if last else layer.tile([P, FEAT_BLOCKS, N], BF16, name="y", tag="y")
             next_h_t = None if last else layer.tile([P, NODE_BLOCKS, H_ROW], BF16, name="h_t", tag="h_t")
-            for p in range(PIECES):
-                piece = slice(p * PIECE, (p + 1) * PIECE)
-                flipped_y = [psum_aux.tile([P, PIECE], y_dtype, name=f"flipped_y{k}", tag="aux") for k in range(FEAT_BLOCKS)]
-                for j in range(BLOCKS_A_PIECE):
-                    y_t = work.tile([P, M], y_dtype, name="y_t", tag=("y_t_last" if last else "y_t"))
-                    aggregate(l, p * BLOCKS_A_PIECE + j, h_t, y_t)
+            y_t, flipped_y = {}, {}
+            for b in range(NODE_BLOCKS + 2):
+                if b < NODE_BLOCKS:
+                    y_t[b] = work.tile([P, M], y_dtype, name="y_t", tag=("y_t_last" if last else "y_t"))
+                    aggregate(l, b, h_t, y_t[b])
+                if 1 <= b <= NODE_BLOCKS:
+                    p, j = divmod(b - 1, BLOCKS_A_PIECE)
+                    piece = slice(p * PIECE, (p + 1) * PIECE)
                     for k in range(FEAT_BLOCKS):
-                        nc.tensor.transpose(flipped_y[k][:, j * P : (j + 1) * P], y_t[:, k * P : (k + 1) * P], y_identity[:])
-                for k in range(FEAT_BLOCKS):
-                    if last:
-                        result = work.tile([P, PIECE], F32, tag="result")
-                        nc.vector.tensor_copy(result[:], flipped_y[k][:])
-                        nc.sync.dma_start(out[k * P : (k + 1) * P, piece], result[:])
-                    else:
-                        nc.vector.tensor_copy(y[:, k, piece], flipped_y[k][:])
-                if not last:
-                    linear(l + 1, p, y, next_h_t)
+                        if j == 0:
+                            flipped_y[k] = psum_aux.tile([P, PIECE], y_dtype, name=f"flipped_y{k}", tag="aux")
+                        nc.tensor.transpose(
+                            flipped_y[k][:, j * P : (j + 1) * P], y_t[b - 1][:, k * P : (k + 1) * P], y_identity[:]
+                        )
+                        if j == BLOCKS_A_PIECE - 1:
+                            target = work.tile([P, PIECE], F32, name="result", tag="result")[:] if last else y[:, k, piece]
+                            if k == 0:
+                                nc.vector.tensor_copy(target, flipped_y[k][:])
+                            else:
+                                nc.scalar.copy(target, flipped_y[k][:])
+                            if last:
+                                nc.sync.dma_start(out[k * P : (k + 1) * P, piece], target)
+                if b >= 2 and (b - 1) % BLOCKS_A_PIECE == 0 and not last:
+                    linear(l + 1, (b - 2) // BLOCKS_A_PIECE, y, next_h_t)
             h_t = next_h_t

@@ -110,20 +110,6 @@ def tile_graphconvlayer_b_kernel(tc, table, w0, b0, adj_t, mask, w1, b1, w2, b2,
 
         scale_t = held.tile([P, NODE_BLOCKS], F32, name="scale_t")
 
-        def aggregate(l, b, h_t, y_t):
-            p, j = divmod(b, BLOCKS_A_PIECE)
-            width = M + 1 if l == 0 else M
-            acc = psum_acc.tile([P, M + 1], F32, tag="acc")
-            for i in range(NODE_BLOCKS):
-                nc.tensor.matmul(
-                    acc[:, 0:width], adj[p][:, i, j * P : (j + 1) * P], h_t[:, i, 0:width],
-                    start=(i == 0), stop=(i == NODE_BLOCKS - 1),
-                )
-            if l == 0:
-                nc.vector.reciprocal(scale_t[:, b : b + 1], acc[:, M : M + 1])
-                nc.vector.tensor_mul(scale_t[:, b : b + 1], scale_t[:, b : b + 1], columns[:, b : b + 1])
-            nc.scalar.activation(y_t[:], acc[:, 0:M], ACT.Gelu, scale=scale_t[:, b : b + 1])
-
         def linear(l, p, y, h_t):
             for b in range(p * BLOCKS_A_PIECE, (p + 1) * BLOCKS_A_PIECE, 2):
                 pair = psum_aux.tile([P, 2, M], F32, tag="aux")
@@ -136,34 +122,70 @@ def tile_graphconvlayer_b_kernel(tc, table, w0, b0, adj_t, mask, w1, b1, w2, b2,
                 bias = biases[l][:].unsqueeze(1).to_broadcast([P, 2, M])
                 nc.vector.tensor_tensor(h_t[:, b : b + 2, 0:M], pair[:], bias, ADD)
 
-        for l in range(LAYERS):
+
+        y = layer.tile([P, FEAT_BLOCKS, N], BF16, tag="y")
+        next_h_t = layer.tile([P, NODE_BLOCKS, H_ROW], BF16, name="h_t", tag="h_t")
+        y_t, flipped_y = {}, {}
+        for b in range(NODE_BLOCKS + 2):
+            if b < NODE_BLOCKS:
+                p, j = divmod(b, BLOCKS_A_PIECE)
+                acc = psum_acc.tile([P, M + 1], F32, tag="acc")
+                for i in range(NODE_BLOCKS):
+                    nc.tensor.matmul(
+                        acc[:], adj[p][:, i, j * P : (j + 1) * P], h_t[:, i, 0 : M + 1],
+                        start=(i == 0), stop=(i == NODE_BLOCKS - 1),
+                    )
+                nc.vector.reciprocal(scale_t[:, b : b + 1], acc[:, M : M + 1])
+                nc.vector.tensor_mul(scale_t[:, b : b + 1], scale_t[:, b : b + 1], columns[:, b : b + 1])
+                y_t[b] = work.tile([P, M], BF16, name="y_t", tag="y_t")
+                nc.scalar.activation(y_t[b][:], acc[:, 0:M], ACT.Gelu, scale=scale_t[:, b : b + 1])
+            if 1 <= b <= NODE_BLOCKS:
+                p, j = divmod(b - 1, BLOCKS_A_PIECE)
+                for k in range(FEAT_BLOCKS):
+                    if j == 0:
+                        flipped_y[k] = psum_aux.tile([P, PIECE], BF16, name=f"flipped_y{k}", tag="aux")
+                    nc.tensor.transpose(
+                        flipped_y[k][:, j * P : (j + 1) * P], y_t[b - 1][:, k * P : (k + 1) * P], identity_bf16[:]
+                    )
+                    if j == BLOCKS_A_PIECE - 1:
+                        if k == 0:
+                            nc.vector.tensor_copy(y[:, k, p * PIECE : (p + 1) * PIECE], flipped_y[k][:])
+                        else:
+                            nc.scalar.copy(y[:, k, p * PIECE : (p + 1) * PIECE], flipped_y[k][:])
+            if b >= 2 and (b - 1) % BLOCKS_A_PIECE == 0:
+                linear(1, (b - 2) // BLOCKS_A_PIECE, y, next_h_t)
+        h_t = next_h_t
+
+        flipped_scale = psum_aux.tile([P, P], F32, tag="aux")
+        nc.tensor.transpose(flipped_scale[0:NODE_BLOCKS, :], scale_t[:], identity_f32[:])
+        scale_rows = held.tile([NODE_BLOCKS, P], F32, name="scale_rows")
+        nc.vector.tensor_copy(scale_rows[:], flipped_scale[0:NODE_BLOCKS, :])
+        nc.sync.dma_start(out[0:1, :].rearrange("o (b q) -> (o b) q", q=P), scale_rows[:])
+        scale_all = held.tile([P, N], F32, name="scale_all")
+        nc.sync.dma_start(scale_all[:], out[0:1, :].rearrange("o n -> (o n)").partition_broadcast(P))
+
+        for l in range(1, LAYERS):
             last = l == LAYERS - 1
-            y_dtype = F32 if last else BF16
-            y_identity = identity_f32 if last else identity_bf16
             y = None if last else layer.tile([P, FEAT_BLOCKS, N], BF16, name="y", tag="y")
             next_h_t = None if last else layer.tile([P, NODE_BLOCKS, H_ROW], BF16, name="h_t", tag="h_t")
-            y_t, flipped_y = {}, {}
-            for b in range(NODE_BLOCKS + 2):
-                if b < NODE_BLOCKS:
-                    y_t[b] = work.tile([P, M], y_dtype, name="y_t", tag=("y_t_last" if last else "y_t"))
-                    aggregate(l, b, h_t, y_t[b])
-                if 1 <= b <= NODE_BLOCKS:
-                    p, j = divmod(b - 1, BLOCKS_A_PIECE)
+            for p in range(PIECES + 1):
+                if p < PIECES:
                     piece = slice(p * PIECE, (p + 1) * PIECE)
                     for k in range(FEAT_BLOCKS):
-                        if j == 0:
-                            flipped_y[k] = psum_aux.tile([P, PIECE], y_dtype, name=f"flipped_y{k}", tag="aux")
-                        nc.tensor.transpose(
-                            flipped_y[k][:, j * P : (j + 1) * P], y_t[b - 1][:, k * P : (k + 1) * P], y_identity[:]
-                        )
-                        if j == BLOCKS_A_PIECE - 1:
-                            target = work.tile([P, PIECE], F32, name="result", tag="result")[:] if last else y[:, k, piece]
-                            if k == 0:
-                                nc.vector.tensor_copy(target, flipped_y[k][:])
-                            else:
-                                nc.scalar.copy(target, flipped_y[k][:])
-                            if last:
-                                nc.sync.dma_start(out[k * P : (k + 1) * P, piece], target)
-                if b >= 2 and (b - 1) % BLOCKS_A_PIECE == 0 and not last:
-                    linear(l + 1, (b - 2) // BLOCKS_A_PIECE, y, next_h_t)
+                        acc = psum_acc.tile([P, PIECE], F32, tag="acc")
+                        for i in range(NODE_BLOCKS):
+                            nc.tensor.matmul(
+                                acc[:], h_t[:, i, k * P : (k + 1) * P], adj[p][:, i, :],
+                                start=(i == 0), stop=(i == NODE_BLOCKS - 1),
+                            )
+                        scaled = work.tile([P, PIECE], F32, tag="scaled")
+                        nc.vector.tensor_mul(scaled[:], acc[:], scale_all[:, piece])
+                        if last:
+                            result = work.tile([P, PIECE], F32, tag="result")
+                            nc.scalar.activation(result[:], scaled[:], ACT.Gelu)
+                            nc.sync.dma_start(out[k * P : (k + 1) * P, piece], result[:])
+                        else:
+                            nc.scalar.activation(y[:, k, piece], scaled[:], ACT.Gelu)
+                if p >= 1 and not last:
+                    linear(l + 1, p - 1, y, next_h_t)
             h_t = next_h_t

@@ -170,22 +170,24 @@ def tile_graphconvlayer_b_kernel(tc, table, w0, b0, adj_t, mask, w1, b1, w2, b2,
             next_h_t = None if last else layer.tile([P, NODE_BLOCKS, H_ROW], BF16, name="h_t", tag="h_t")
             for p in range(PIECES + 1):
                 if p < PIECES:
-                    piece = slice(p * PIECE, (p + 1) * PIECE)
-                    for k in range(FEAT_BLOCKS):
-                        acc = psum_acc.tile([P, PIECE], F32, tag="acc")
-                        for i in range(NODE_BLOCKS):
-                            nc.tensor.matmul(
-                                acc[:], h_t[:, i, k * P : (k + 1) * P], adj[p][:, i, :],
-                                start=(i == 0), stop=(i == NODE_BLOCKS - 1),
-                            )
-                        scaled = work.tile([P, PIECE], F32, tag="scaled")
-                        nc.vector.tensor_mul(scaled[:], acc[:], scale_all[:, piece])
-                        if last:
-                            result = work.tile([P, PIECE], F32, tag="result")
-                            nc.scalar.activation(result[:], scaled[:], ACT.Gelu)
-                            nc.sync.dma_start(out[k * P : (k + 1) * P, piece], result[:])
-                        else:
-                            nc.scalar.activation(y[:, k, piece], scaled[:], ACT.Gelu)
+                    width = PIECE // 4 if last and p == PIECES - 1 else PIECE
+                    for c in range(0, PIECE, width):
+                        columns_here = slice(p * PIECE + c, p * PIECE + c + width)
+                        for k in range(FEAT_BLOCKS):
+                            acc = psum_acc.tile([P, PIECE], F32, tag="acc")
+                            for i in range(NODE_BLOCKS):
+                                nc.tensor.matmul(
+                                    acc[:, 0:width], h_t[:, i, k * P : (k + 1) * P], adj[p][:, i, c : c + width],
+                                    start=(i == 0), stop=(i == NODE_BLOCKS - 1),
+                                )
+                            scaled = work.tile([P, PIECE], F32, tag="scaled")
+                            nc.vector.tensor_mul(scaled[:, 0:width], acc[:, 0:width], scale_all[:, columns_here])
+                            if last:
+                                result = work.tile([P, PIECE], F32, tag="result")
+                                nc.scalar.activation(result[:, 0:width], scaled[:, 0:width], ACT.Gelu)
+                                nc.sync.dma_start(out[k * P : (k + 1) * P, columns_here], result[:, 0:width])
+                            else:
+                                nc.scalar.activation(y[:, k, columns_here], scaled[:, 0:width], ACT.Gelu)
                 if p >= 1 and not last:
                     linear(l + 1, p - 1, y, next_h_t)
             h_t = next_h_t

import concourse.mybir as mybir
from concourse.masks import make_identity

BF16, F32, U16 = mybir.dt.bfloat16, mybir.dt.float32, mybir.dt.uint16
ACT = mybir.ActivationFunctionType
ADD = mybir.AluOpType.add

P = 128
S = 4096
M = 256
N = 2048
PIECE = 512
WORD_BLOCKS = S // P
NODE_BLOCKS = N // P
FEAT_BLOCKS = M // P
PIECES = N // PIECE
BLOCKS_A_PIECE = PIECE // P
LAYERS = 3
H_ROW = 272

FLOPS = 2 * P * M * N + 2 * 2 * M * M * N + LAYERS * 2 * M * N * N


def tile_graphconvlayer_b_kernel(tc, table, w0, b0, adj_t, mask, w1, b1, w2, b2, offs, out):
    nc = tc.nc
    with (
        tc.tile_pool(name="held", bufs=1) as held,
        tc.tile_pool(name="layer", bufs=2) as layer,
        tc.tile_pool(name="work", bufs=4) as work,
        tc.psum_pool(name="psum_acc", bufs=4) as psum_acc,
        tc.psum_pool(name="psum_aux", bufs=4) as psum_aux,
    ):
        table_rows = held.tile([P, WORD_BLOCKS, P], BF16, name="table_rows")
        table_blocks = table.rearrange("(b q) d -> q b d", q=P)
        for g in range(WORD_BLOCKS // 4):
            nc.sync.dma_start(table_rows[:, 4 * g : 4 * g + 4, :], table_blocks[:, 4 * g : 4 * g + 4, :])

        offsets = held.tile([P, N // 16], U16, name="offsets")
        nc.sync.dma_start(offsets[:], offs)

        rows = held.tile([P, P], F32, name="rows")
        nc.vector.memset(rows[:], 0.0)
        nc.sync.dma_start(rows[0:NODE_BLOCKS, :], mask.rearrange("o (b q) -> (o b) q", q=P))
        nc.sync.dma_start(rows[NODE_BLOCKS : NODE_BLOCKS + FEAT_BLOCKS, :], b0.rearrange("(e q) o -> e (q o)", q=P))

        w0_sb = held.tile([P, M], BF16, name="w0_sb")
        nc.sync.dma_start(w0_sb[:], w0)

        adj = [held.tile([P, NODE_BLOCKS, PIECE], BF16, name=f"adj{p}") for p in range(PIECES)]
        adj_blocks = adj_t.rearrange("(b q) n -> q b n", q=P)

        def load_adj(p):
            for g in range(4):
                nc.sync.dma_start(
                    adj[p][:, 4 * g : 4 * g + 4, :],
                    adj_blocks[:, 4 * g : 4 * g + 4, p * PIECE : (p + 1) * PIECE],
                )

        load_adj(0)
        load_adj(1)
        weights, biases = {}, {}
        for l, (w, b) in ((1, (w1, b1)), (2, (w2, b2))):
            weights[l] = held.tile([P, FEAT_BLOCKS, M], BF16, name=f"w{l}_sb")
            nc.sync.dma_start(weights[l][:], w.rearrange("(k q) e -> q k e", q=P))
            biases[l] = held.tile([P, M], F32, name=f"b{l}_all")
            nc.sync.dma_start(biases[l][:], b.rearrange("m o -> (m o)").partition_broadcast(P))
            load_adj(l + 1)

        identity_bf16 = held.tile([P, P], BF16, name="identity_bf16")
        make_identity(nc, identity_bf16[:])
        identity_f32 = held.tile([P, P], F32, name="identity_f32")
        make_identity(nc, identity_f32[:])

        table_t = held.tile([P, S], BF16, name="table_t")
        for g in range(WORD_BLOCKS // 4):
            flipped_words = psum_aux.tile([P, 4 * P], BF16, tag="aux")
            for k in range(4):
                nc.tensor.transpose(flipped_words[:, k * P : (k + 1) * P], table_rows[:, 4 * g + k, :], identity_bf16[:])
            if g % 2 == 0:
                nc.vector.tensor_copy(table_t[:, g * 4 * P : (g + 1) * 4 * P], flipped_words[:])
            else:
                nc.scalar.copy(table_t[:, g * 4 * P : (g + 1) * 4 * P], flipped_words[:])

        flipped_rows = psum_aux.tile([P, P], F32, tag="aux")
        nc.tensor.transpose(flipped_rows[:], rows[:], identity_f32[:])
        columns = held.tile([P, NODE_BLOCKS + FEAT_BLOCKS], F32, name="columns")
        nc.vector.tensor_copy(columns[:], flipped_rows[:, 0 : NODE_BLOCKS + FEAT_BLOCKS])

        h_t = layer.tile([P, NODE_BLOCKS, H_ROW], BF16, tag="h_t")
        nc.vector.memset(h_t[:, :, M : M + 1], 1.0)
        h0 = {}
        for p in range(PIECES + 1):
            if p < PIECES:
                for e in range(FEAT_BLOCKS):
                    looked_up = table_t[:].indirect(offsets[:, p * (PIECE // 16) : (p + 1) * (PIECE // 16)])
                    product = psum_acc.tile([P, PIECE], F32, tag="acc")
                    nc.tensor.matmul(product[:], w0_sb[:, e * P : (e + 1) * P], looked_up, start=True, stop=True)
                    h0[p, e] = work.tile([P, PIECE], BF16, name="h0", tag="h0")
                    nc.scalar.activation(
                        h0[p, e][:], product[:], ACT.Identity, bias=columns[:, NODE_BLOCKS + e : NODE_BLOCKS + e + 1]
                    )
            if p >= 1:
                flipped_h = psum_aux.tile([P, BLOCKS_A_PIECE, M], BF16, tag="aux")
                for e in range(FEAT_BLOCKS):
                    for k in range(BLOCKS_A_PIECE):
                        nc.tensor.transpose(
                            flipped_h[:, k, e * P : (e + 1) * P], h0[p - 1, e][:, k * P : (k + 1) * P], identity_bf16[:]
                        )
                nc.vector.tensor_copy(h_t[:, (p - 1) * BLOCKS_A_PIECE : p * BLOCKS_A_PIECE, 0:M], flipped_h[:])

        scale_t = held.tile([P, NODE_BLOCKS], F32, name="scale_t")

        def linear(l, p, y, h_t):
            for b in range(p * BLOCKS_A_PIECE, (p + 1) * BLOCKS_A_PIECE, 2):
                pair = psum_aux.tile([P, 2, M], F32, tag="aux")
                for i in range(2):
                    for k in range(FEAT_BLOCKS):
                        nc.tensor.matmul(
                            pair[:, i, :], y[:, k, (b + i) * P : (b + i + 1) * P], weights[l][:, k, :],
                            start=(k == 0), stop=(k == FEAT_BLOCKS - 1),
                        )
                bias = biases[l][:].unsqueeze(1).to_broadcast([P, 2, M])
                nc.vector.tensor_tensor(h_t[:, b : b + 2, 0:M], pair[:], bias, ADD)


        y = layer.tile([P, FEAT_BLOCKS, N], BF16, tag="y")
        next_h_t = layer.tile([P, NODE_BLOCKS, H_ROW], BF16, name="h_t", tag="h_t")
        y_t, flipped_y = {}, {}
        for b in range(NODE_BLOCKS + 2):
            if b < NODE_BLOCKS:
                p, j = divmod(b, BLOCKS_A_PIECE)
                acc = psum_acc.tile([P, M + 1], F32, tag="acc")
                for i in range(NODE_BLOCKS):
                    nc.tensor.matmul(
                        acc[:], adj[p][:, i, j * P : (j + 1) * P], h_t[:, i, 0 : M + 1],
                        start=(i == 0), stop=(i == NODE_BLOCKS - 1),
                    )
                nc.vector.reciprocal(scale_t[:, b : b + 1], acc[:, M : M + 1])
                nc.vector.tensor_mul(scale_t[:, b : b + 1], scale_t[:, b : b + 1], columns[:, b : b + 1])
                y_t[b] = work.tile([P, M], BF16, name="y_t", tag="y_t")
                nc.scalar.activation(y_t[b][:], acc[:, 0:M], ACT.Gelu, scale=scale_t[:, b : b + 1])
            if 1 <= b <= NODE_BLOCKS:
                p, j = divmod(b - 1, BLOCKS_A_PIECE)
                for k in range(FEAT_BLOCKS):
                    if j == 0:
                        flipped_y[k] = psum_aux.tile([P, PIECE], BF16, name=f"flipped_y{k}", tag="aux")
                    nc.tensor.transpose(
                        flipped_y[k][:, j * P : (j + 1) * P], y_t[b - 1][:, k * P : (k + 1) * P], identity_bf16[:]
                    )
                    if j == BLOCKS_A_PIECE - 1:
                        if k == 0:
                            nc.vector.tensor_copy(y[:, k, p * PIECE : (p + 1) * PIECE], flipped_y[k][:])
                        else:
                            nc.scalar.copy(y[:, k, p * PIECE : (p + 1) * PIECE], flipped_y[k][:])
            if b >= 2 and (b - 1) % BLOCKS_A_PIECE == 0:
                linear(1, (b - 2) // BLOCKS_A_PIECE, y, next_h_t)
        h_t = next_h_t

        flipped_scale = psum_aux.tile([P, P], F32, tag="aux")
        nc.tensor.transpose(flipped_scale[0:NODE_BLOCKS, :], scale_t[:], identity_f32[:])
        scale_rows = held.tile([NODE_BLOCKS, P], F32, name="scale_rows")
        nc.vector.tensor_copy(scale_rows[:], flipped_scale[0:NODE_BLOCKS, :])
        nc.sync.dma_start(out[0:1, :].rearrange("o (b q) -> (o b) q", q=P), scale_rows[:])
        scale_all = held.tile([P, N], F32, name="scale_all")
        nc.sync.dma_start(scale_all[:], out[0:1, :].rearrange("o n -> (o n)").partition_broadcast(P))

        for l in range(1, LAYERS):
            last = l == LAYERS - 1
            y = None if last else layer.tile([P, FEAT_BLOCKS, N], BF16, name="y", tag="y")
            next_h_t = None if last else layer.tile([P, NODE_BLOCKS, H_ROW], BF16, name="h_t", tag="h_t")
            for p in range(PIECES + 1):
                if p < PIECES:
                    width = PIECE // 4 if last and p == PIECES - 1 else PIECE
                    for c in range(0, PIECE, width):
                        columns_here = slice(p * PIECE + c, p * PIECE + c + width)
                        for k in range(FEAT_BLOCKS):
                            acc = psum_acc.tile([P, PIECE], F32, tag="acc")
                            for i in range(NODE_BLOCKS):
                                nc.tensor.matmul(
                                    acc[:, 0:width], h_t[:, i, k * P : (k + 1) * P], adj[p][:, i, c : c + width],
                                    start=(i == 0), stop=(i == NODE_BLOCKS - 1),
                                )
                            scaled = work.tile([P, PIECE], F32, tag="scaled")
                            nc.vector.tensor_mul(scaled[:, 0:width], acc[:, 0:width], scale_all[:, columns_here])
                            if last:
                                result = work.tile([P, PIECE], F32, tag="result")
                                nc.scalar.activation(result[:, 0:width], scaled[:, 0:width], ACT.Gelu)
                                nc.sync.dma_start(out[k * P : (k + 1) * P, columns_here], result[:, 0:width])
                            else:
                                nc.scalar.activation(y[:, k, columns_here], scaled[:, 0:width], ACT.Gelu)
                if p >= 1 and not last:
                    linear(l + 1, p - 1, y, next_h_t)
            h_t = next_h_t
